import numpy as np
import ml_dtypes


def mxq(x, axis, fmt="e4m3"):
    dtype, down = {"e4m3": (ml_dtypes.float8_e4m3fn, 7), "e5m2": (ml_dtypes.float8_e5m2, 14)}[fmt]
    v = np.moveaxis(np.asarray(x, np.float32).astype(ml_dtypes.bfloat16).astype(np.float64), axis, -1)
    blocks = v.reshape(v.shape[:-1] + (-1, 32))
    amax = np.abs(blocks).max(-1, keepdims=True)
    byte = np.maximum(np.where(amax > 0, np.frexp(amax)[1] - 1 + 127, 0) - down, 1)
    scale = np.exp2(byte - 127.0)
    codes = (blocks / scale).astype(np.float32).astype(dtype).astype(np.float64)
    return np.moveaxis((codes * scale).reshape(v.shape), -1, axis)


WIDE = False


def mx_kscale(k):
    if not WIDE:
        return np.ones(k)
    levels = np.array([10, -10, 5, -5, 0])
    a = np.random.permutation(np.resize(levels, k // 512 * 4)).reshape(k // 512, 4)
    idx = np.arange(k)
    return np.exp2(a[idx // 512, idx % 128 // 32])


BF16 = ml_dtypes.bfloat16


def bf(x):
    return np.asarray(x, np.float32).astype(BF16)


def f64(x):
    return np.asarray(x).astype(np.float64)


B, H, C, W = 2, 64, 1024, 512
EPS = 1e-8
MASK_MIN = 0.0


def setup_inputs():
    s = mx_kscale(W)
    rows = 0.5 + 1.5 * np.random.random_sample((B, C, 1))
    return {"memory": bf(np.random.standard_normal((B, C, W)) * rows * s),
            "keys": bf(np.random.standard_normal((B, H, W)) * s),
            "betas": bf(np.sqrt(W) * (0.6 + 0.6 * np.random.random_sample((B, H)))),
            "mask": bf(np.random.random_sample((B, H, W)) / s)}


def reference(memory, keys, betas, mask):
    memory, keys, betas = f64(memory), f64(keys), f64(betas)
    mask = f64(mask) * (1.0 - MASK_MIN) + MASK_MIN
    m2 = mask * mask
    keys_m = keys * mask
    dots = mxq(keys * m2, 2, "e4m3") @ mxq(memory, 2, "e4m3").transpose(0, 2, 1)
    keys_norm = np.sqrt((keys_m * keys_m).sum(-1))
    mem_norm = np.sqrt(mxq(m2, 2, "e4m3") @ mxq(memory * memory, 2, "e4m3").transpose(0, 2, 1))
    norm = keys_norm[..., None] * mem_norm
    scores = dots / (norm + EPS) * betas[..., None]
    e = np.exp(scores - scores.max(-1, keepdims=True))
    return e / e.sum(-1, keepdims=True)

@@ -1,0 +1,194 @@
+from contextlib import ExitStack
+
+import concourse.mybir as mybir
+from concourse.masks import make_identity
+
+F32 = mybir.dt.float32
+BF16 = mybir.dt.bfloat16
+I32 = mybir.dt.int32
+U32 = mybir.dt.uint32
+U8 = mybir.dt.uint8
+FP8X4 = mybir.dt.float8_e4m3fn_x4
+ACT = mybir.ActivationFunctionType
+ALU = mybir.AluOpType
+AXIS = mybir.AxisListType
+
+B, H, C, W = 2, 64, 1024, 512
+P = 128
+PACK = 4
+EPS = 1e-8
+GUARD = 1e-26
+
+T = 2
+CELLS = T * P
+CHUNKS = C // CELLS
+WORDS = W // 2
+
+FLOPS = 2 * 2 * B * H * C * W
+
+assert B * H == P and W == P * PACK
+
+
+def tile_contentaddressing_s_kernel(tc, memory, keys, betas, mask, out):
+    nc = tc.nc
+    with ExitStack() as stack:
+        const = stack.enter_context(tc.tile_pool(name="const", bufs=1))
+        chunk = stack.enter_context(tc.tile_pool(name="chunk", bufs=CHUNKS))
+        flip = stack.enter_context(tc.psum_pool(name="flip", bufs=4))
+        sums = stack.enter_context(tc.psum_pool(name="sums", bufs=CHUNKS))
+
+        ident = const.tile([P, P], F32)
+        make_identity(nc, ident[:])
+        guard = const.tile([P, 1], F32)
+        nc.vector.memset(guard[:], GUARD)
+        first_table = const.tile([P, 1], F32)
+        nc.scalar.activation(out=first_table[:], in_=guard[:], func=ACT.Abs_reciprocal_sqrt)
+
+        mask_sb = const.tile([P, W], BF16)
+        keys_sb = const.tile([P, W], BF16)
+        nc.sync.dma_start(out=mask_sb[:], in_=mask.rearrange("b h w -> (b h) w"))
+        nc.sync.dma_start(out=keys_sb[:], in_=keys.rearrange("b h w -> (b h) w"))
+        beta_bf = const.tile([P, 1], BF16)
+        with nc.allow_non_contiguous_dma(reason="one beta for each partition, 128 in all"):
+            nc.scalar.dma_start(out=beta_bf[:], in_=betas.rearrange("b (h o) -> (b h) o", o=1))
+        mem_view = memory.rearrange("b (q j t) w -> q j b (t w)", q=CHUNKS, j=P, t=T)
+        cells_sb = []
+        for q in range(CHUNKS):
+            x = chunk.tile([P, B, T * W], BF16, name="x")
+            nc.sync.dma_start(out=x[:], in_=mem_view[q])
+            cells_sb.append(x)
+
+        m2 = const.tile([P, W], F32)
+        nc.vector.tensor_mul(out=m2[:], in0=mask_sb[:], in1=mask_sb[:])
+        km2 = const.tile([P, W], F32)
+        nc.vector.tensor_mul(out=km2[:], in0=keys_sb[:], in1=m2[:])
+        km = const.tile([P, W], F32)
+        nc.vector.tensor_mul(out=km[:], in0=keys_sb[:], in1=mask_sb[:])
+        beta = const.tile([P, 1], F32)
+        nc.vector.tensor_copy(out=beta[:], in_=beta_bf[:])
+
+        km_sq = const.tile([P, W], F32)
+        kn_sq = const.tile([P, 1], F32)
+        nc.scalar.activation(out=km_sq[:], in_=km[:], func=ACT.Square, accum_out=kn_sq[:])
+        kn_inv = const.tile([P, 1], F32)
+        nc.scalar.activation(
+            out=kn_inv[:], in_=kn_sq[:], func=ACT.Abs_reciprocal_sqrt, bias=guard[:]
+        )
+        keys_norm = const.tile([P, 1], F32)
+        nc.vector.reciprocal(out=keys_norm[:], in_=kn_inv[:])
+
+        head_vals = const.tile([P, 2 * B * 2 * H * PACK], BF16, align_bytes=64)
+        nc.vector.memset(head_vals[:].bitcast(I32), 0)
+        head_view = head_vals[:].rearrange(
+            "p (o a z h t) -> p o a z h t", o=2, a=B, z=2, h=H, t=PACK
+        )
+        for o, rows in enumerate((km2, m2)):
+            turned = flip.tile([P, PACK, P], F32, name="turned")
+            by_word = rows[:].rearrange("r (u p e) -> r u e p", u=2, e=2)
+            for u in range(2):
+                for e in range(2):
+                    nc.tensor.transpose(turned[:, 2 * u + e, :], by_word[:, u, e, :], ident[:])
+            src = turned[:].rearrange("p t (a h) -> p a h t", a=B)
+            if o == 0:
+                nc.vector.tensor_copy(out=head_view[:, o, :, 0, :, :], in_=src)
+            else:
+                nc.scalar.copy(out=head_view[:, o, :, 0, :, :], in_=src)
+        head_codes = const.tile([P, 2 * B * 2 * H], U32, align_bytes=64)
+        head_scales = const.tile([P, 2 * B * 2 * H], U8, align_bytes=64)
+        nc.vector.quantize_mx(
+            out=head_codes[:].bitcast(FP8X4), scales=head_scales[:], in_=head_vals[:]
+        )
+
+        scores = const.tile([P, C], F32)
+        chunk_max = const.tile([P, CHUNKS], F32)
+        next_table = const.tile([P, 1], F32)
+
+        for q in range(CHUNKS):
+            words = cells_sb[q][:].bitcast(F32)
+            mem_vals = chunk.tile([P, B, P, T * PACK], BF16, name="mem_vals", align_bytes=64)
+            sq_vals = chunk.tile([P, B, P, T * PACK], BF16, name="sq_vals", align_bytes=64)
+            for b in range(B):
+                turned = flip.tile([P, PACK, P], F32, name="turned")
+                for m in range(T * 2):
+                    nc.tensor.transpose(
+                        turned[:, m, :], words[:, b, m * P : (m + 1) * P], ident[:]
+                    )
+                nc.scalar.copy(
+                    out=mem_vals[:].bitcast(F32)[:, b, :, :],
+                    in_=turned[:].rearrange("p m j -> p j m"),
+                )
+                if b == 0:
+                    nc.vector.tensor_mul(
+                        out=sq_vals[:, b, :, :], in0=mem_vals[:, b, :, :], in1=mem_vals[:, b, :, :]
+                    )
+                else:
+                    nc.scalar.activation(
+                        out=sq_vals[:, b, :, :].rearrange("p j (m e) -> p j m e", e=2),
+                        in_=turned[:].bitcast(BF16).rearrange("p m (j e) -> p j m e", e=2),
+                        func=ACT.Square,
+                    )
+
+            acc = sums.tile([P, 2, CELLS], F32, name="acc")
+            for o, vals in enumerate((mem_vals, sq_vals)):
+                codes = chunk.tile([P, B * CELLS], U32, name="codes%d" % o, align_bytes=64)
+                scales = chunk.tile([P, B * CELLS], U8, name="scales%d" % o, align_bytes=64)
+                nc.vector.quantize_mx(
+                    out=codes[:].bitcast(FP8X4),
+                    scales=scales[:],
+                    in_=vals[:].rearrange("p b j v -> p (b j v)"),
+                )
+                for b in range(B):
+                    heads = slice(o * 4 * H + b * H, o * 4 * H + b * H + P)
+                    cols = slice(b * CELLS, (b + 1) * CELLS)
+                    nc.tensor.matmul_mx(
+                        out=acc[:, o, :],
+                        lhsT=head_codes[:, heads].bitcast(FP8X4),
+                        lhsT_scale=head_scales[:, heads],
+                        rhs=codes[:, cols].bitcast(FP8X4),
+                        rhs_scale=scales[:, cols],
+                        start=(b == 0),
+                        stop=(b == B - 1),
+                    )
+
+            a = chunk.tile([P, CELLS], F32, name="a")
+            nc.scalar.activation(
+                out=a[:], in_=acc[:, 1, :], func=ACT.Abs_reciprocal_sqrt, bias=guard[:]
+            )
+            den_sq = chunk.tile([P, CELLS], F32, name="den_sq")
+            nc.scalar.activation(
+                out=den_sq[:], in_=a[:], func=ACT.Square, scale=EPS, bias=keys_norm[:]
+            )
+            u = chunk.tile([P, CELLS], F32, name="u")
+            nc.scalar.activation(out=u[:], in_=den_sq[:], func=ACT.Abs_reciprocal_sqrt)
+            if q == CHUNKS - 1:
+                nc.scalar.activation(out=next_table[:], in_=u[:, 0:1], func=ACT.Exp)
+            cosine = chunk.tile([P, CELLS], F32, name="cosine")
+            nc.vector.scalar_tensor_tensor(
+                out=cosine[:], in0=acc[:, 0, :], scalar=beta[:, 0:1], in1=a[:],
+                op0=ALU.mult, op1=ALU.mult,
+            )
+            cols = slice(q * CELLS, (q + 1) * CELLS)
+            nc.vector.tensor_mul(out=scores[:, cols], in0=cosine[:], in1=u[:])
+            nc.vector.tensor_reduce(
+                out=chunk_max[:, q : q + 1], in_=scores[:, cols], axis=AXIS.X, op=ALU.max
+            )
+
+        neg_max = const.tile([P, 1], F32)
+        nc.vector.tensor_reduce(
+            out=neg_max[:], in_=chunk_max[:], axis=AXIS.X, op=ALU.max, negate=True
+        )
+        expd = const.tile([P, C], F32)
+        total = const.tile([P, 1], F32)
+        nc.scalar.activation(
+            out=expd[:], in_=scores[:], func=ACT.Exp, bias=neg_max[:], accum_out=total[:]
+        )
+        inv_total = const.tile([P, 1], F32)
+        nc.vector.reciprocal(out=inv_total[:], in_=total[:])
+        out_rows = out.rearrange("b h c -> (b h) c")
+        half = C // 2
+        left = const.tile([P, half], F32)
+        nc.vector.tensor_scalar_mul(out=left[:], in0=expd[:, 0:half], scalar1=inv_total[:, 0:1])
+        nc.sync.dma_start(out=out_rows[:, 0:half], in_=left[:])
+        right = const.tile([P, half], F32)
+        nc.scalar.activation(out=right[:], in_=expd[:, half:C], func=ACT.Copy, scale=inv_total[:, 0:1])
+        nc.scalar.dma_start(out=out_rows[:, half:C], in_=right[:])

@@ -22,7 +22,9 @@ GUARD = 1e-26
 T = 2
 CELLS = T * P
 CHUNKS = C // CELLS
-WORDS = W // 2
+LAST = CHUNKS - 1
+TURN_AHEAD = 2
+VECTOR_COLS = 640
 
 FLOPS = 2 * 2 * B * H * C * W
 
@@ -34,8 +36,13 @@ def tile_contentaddressing_s_kernel(tc, memory, keys, betas, mask, out):
     with ExitStack() as stack:
         const = stack.enter_context(tc.tile_pool(name="const", bufs=1))
         chunk = stack.enter_context(tc.tile_pool(name="chunk", bufs=CHUNKS))
-        flip = stack.enter_context(tc.psum_pool(name="flip", bufs=4))
+        flip = stack.enter_context(tc.psum_pool(name="flip", bufs=2 * TURN_AHEAD))
         sums = stack.enter_context(tc.psum_pool(name="sums", bufs=CHUNKS))
+        stack.enter_context(tc.manual_schedule())
+
+        beta_bf = const.tile([P, 1], BF16)
+        with nc.allow_non_contiguous_dma(reason="one beta for each partition, 128 in all"):
+            nc.scalar.dma_start(out=beta_bf[:], in_=betas.rearrange("b (h o) -> (b h) o", o=1))
 
         ident = const.tile([P, P], F32)
         make_identity(nc, ident[:])
@@ -43,20 +50,97 @@ def tile_contentaddressing_s_kernel(tc, memory, keys, betas, mask, out):
         nc.vector.memset(guard[:], GUARD)
         first_table = const.tile([P, 1], F32)
         nc.scalar.activation(out=first_table[:], in_=guard[:], func=ACT.Abs_reciprocal_sqrt)
+        head_vals = const.tile([P, 2 * B * 2 * H * PACK], BF16, align_bytes=64)
+        nc.vector.memset(head_vals[:].bitcast(I32), 0)
 
+        mem_view = memory.rearrange("b (q j t) w -> q j b (t w)", q=CHUNKS, j=P, t=T)
+        cells_sb = [chunk.tile([P, B, T * W], BF16, name="x") for q in range(CHUNKS)]
         mask_sb = const.tile([P, W], BF16)
         keys_sb = const.tile([P, W], BF16)
+        nc.sync.dma_start(out=cells_sb[0][:, 0, :], in_=mem_view[0][:, 0, :])
         nc.sync.dma_start(out=mask_sb[:], in_=mask.rearrange("b h w -> (b h) w"))
         nc.sync.dma_start(out=keys_sb[:], in_=keys.rearrange("b h w -> (b h) w"))
-        beta_bf = const.tile([P, 1], BF16)
-        with nc.allow_non_contiguous_dma(reason="one beta for each partition, 128 in all"):
-            nc.scalar.dma_start(out=beta_bf[:], in_=betas.rearrange("b (h o) -> (b h) o", o=1))
-        mem_view = memory.rearrange("b (q j t) w -> q j b (t w)", q=CHUNKS, j=P, t=T)
-        cells_sb = []
-        for q in range(CHUNKS):
-            x = chunk.tile([P, B, T * W], BF16, name="x")
-            nc.sync.dma_start(out=x[:], in_=mem_view[q])
-            cells_sb.append(x)
+        nc.sync.dma_start(out=cells_sb[0][:, 1, :], in_=mem_view[0][:, 1, :])
+        for q in range(1, CHUNKS):
+            nc.sync.dma_start(out=cells_sb[q][:], in_=mem_view[q])
+
+        mem_vals = [
+            chunk.tile([P, B, P, T * PACK], BF16, name="mem_vals", align_bytes=64)
+            for q in range(CHUNKS)
+        ]
+        codes = {}
+        scales = {}
+        acc = {}
+        inv_mem = const.tile([P, C], F32)
+        den_sq = const.tile([P, C], F32)
+        inv_den = const.tile([P, C], F32)
+        cosine = const.tile([P, C], F32)
+        scores = const.tile([P, C + 1], F32)
+
+        def turn(q):
+            words = cells_sb[q][:].bitcast(F32)
+            for b in range(B):
+                turned = flip.tile([P, PACK, P], F32, name="turned")
+                for m in range(T * 2):
+                    nc.tensor.transpose(
+                        turned[:, m, :], words[:, b, m * P : (m + 1) * P], ident[:]
+                    )
+                nc.scalar.copy(
+                    out=mem_vals[q][:].bitcast(F32)[:, b, :, :],
+                    in_=turned[:].rearrange("p m j -> p j m"),
+                )
+
+        def square_and_quantise(q):
+            flat = mem_vals[q][:].rearrange("p b j v -> p (b j v)")
+            sq_vals = chunk.tile([P, B * CELLS * PACK], BF16, name="sq_vals", align_bytes=64)
+            nc.vector.tensor_mul(out=sq_vals[:], in0=flat, in1=flat)
+            for o, vals in enumerate((flat, sq_vals[:])):
+                codes[q, o] = chunk.tile([P, B * CELLS], U32, name="codes%d" % o, align_bytes=64)
+                scales[q, o] = chunk.tile([P, B * CELLS], U8, name="scales%d" % o, align_bytes=64)
+                nc.vector.quantize_mx(
+                    out=codes[q, o][:].bitcast(FP8X4), scales=scales[q, o][:], in_=vals
+                )
+
+        def multiply(q):
+            acc[q] = sums.tile([P, 2, CELLS], F32, name="acc")
+            for o in range(2):
+                for b in range(B):
+                    heads = slice(o * 4 * H + b * H, o * 4 * H + b * H + P)
+                    cols = slice(b * CELLS, (b + 1) * CELLS)
+                    nc.tensor.matmul_mx(
+                        out=acc[q][:, o, :],
+                        lhsT=head_codes[:, heads].bitcast(FP8X4),
+                        lhsT_scale=head_scales[:, heads],
+                        rhs=codes[q, o][:, cols].bitcast(FP8X4),
+                        rhs_scale=scales[q, o][:, cols],
+                        start=(b == 0),
+                        stop=(b == B - 1),
+                    )
+
+        def inverse_mem_norm(q):
+            nc.scalar.activation(
+                out=inv_mem[:, q * CELLS : (q + 1) * CELLS], in_=acc[q][:, 1, :],
+                func=ACT.Abs_reciprocal_sqrt, bias=guard[:],
+            )
+
+        def score(first, stop):
+            cols = slice(first * CELLS, stop * CELLS)
+            nc.scalar.activation(
+                out=den_sq[:, cols], in_=inv_mem[:, cols], func=ACT.Square,
+                scale=EPS, bias=keys_norm[:],
+            )
+            nc.scalar.activation(
+                out=inv_den[:, cols], in_=den_sq[:, cols], func=ACT.Abs_reciprocal_sqrt
+            )
+            for q in range(first, stop):
+                own = slice(q * CELLS, (q + 1) * CELLS)
+                nc.vector.scalar_tensor_tensor(
+                    out=cosine[:, own], in0=acc[q][:, 0, :], scalar=beta[:, 0:1],
+                    in1=inv_mem[:, own], op0=ALU.mult, op1=ALU.mult,
+                )
+            nc.vector.tensor_mul(out=scores[:, cols], in0=cosine[:, cols], in1=inv_den[:, cols])
+
+        turn(0)
 
         m2 = const.tile([P, W], F32)
         nc.vector.tensor_mul(out=m2[:], in0=mask_sb[:], in1=mask_sb[:])
@@ -64,8 +148,20 @@ def tile_contentaddressing_s_kernel(tc, memory, keys, betas, mask, out):
         nc.vector.tensor_mul(out=km2[:], in0=keys_sb[:], in1=m2[:])
         km = const.tile([P, W], F32)
         nc.vector.tensor_mul(out=km[:], in0=keys_sb[:], in1=mask_sb[:])
-        beta = const.tile([P, 1], F32)
-        nc.vector.tensor_copy(out=beta[:], in_=beta_bf[:])
+
+        head_view = head_vals[:].rearrange(
+            "p (o a z h t) -> p o a z h t", o=2, a=B, z=2, h=H, t=PACK
+        )
+        for o, rows in ((1, m2), (0, km2)):
+            turned = flip.tile([P, PACK, P], F32, name="turned")
+            by_word = rows[:].rearrange("r (u p e) -> r u e p", u=2, e=2)
+            for u in range(2):
+                for e in range(2):
+                    nc.tensor.transpose(turned[:, 2 * u + e, :], by_word[:, u, e, :], ident[:])
+            nc.scalar.copy(
+                out=head_view[:, o, :, 0, :, :],
+                in_=turned[:].rearrange("p t (a h) -> p a h t", a=B),
+            )
 
         km_sq = const.tile([P, W], F32)
         kn_sq = const.tile([P, 1], F32)
@@ -74,121 +170,54 @@ def tile_contentaddressing_s_kernel(tc, memory, keys, betas, mask, out):
         nc.scalar.activation(
             out=kn_inv[:], in_=kn_sq[:], func=ACT.Abs_reciprocal_sqrt, bias=guard[:]
         )
-        keys_norm = const.tile([P, 1], F32)
-        nc.vector.reciprocal(out=keys_norm[:], in_=kn_inv[:])
 
-        head_vals = const.tile([P, 2 * B * 2 * H * PACK], BF16, align_bytes=64)
-        nc.vector.memset(head_vals[:].bitcast(I32), 0)
-        head_view = head_vals[:].rearrange(
-            "p (o a z h t) -> p o a z h t", o=2, a=B, z=2, h=H, t=PACK
-        )
-        for o, rows in enumerate((km2, m2)):
-            turned = flip.tile([P, PACK, P], F32, name="turned")
-            by_word = rows[:].rearrange("r (u p e) -> r u e p", u=2, e=2)
-            for u in range(2):
-                for e in range(2):
-                    nc.tensor.transpose(turned[:, 2 * u + e, :], by_word[:, u, e, :], ident[:])
-            src = turned[:].rearrange("p t (a h) -> p a h t", a=B)
-            if o == 0:
-                nc.vector.tensor_copy(out=head_view[:, o, :, 0, :, :], in_=src)
-            else:
-                nc.scalar.copy(out=head_view[:, o, :, 0, :, :], in_=src)
+        turn(1)
+        square_and_quantise(0)
         head_codes = const.tile([P, 2 * B * 2 * H], U32, align_bytes=64)
         head_scales = const.tile([P, 2 * B * 2 * H], U8, align_bytes=64)
         nc.vector.quantize_mx(
             out=head_codes[:].bitcast(FP8X4), scales=head_scales[:], in_=head_vals[:]
         )
+        keys_norm = const.tile([P, 1], F32)
+        nc.vector.reciprocal(out=keys_norm[:], in_=kn_inv[:])
+        beta = const.tile([P, 1], F32)
+        nc.vector.tensor_copy(out=beta[:], in_=beta_bf[:])
 
-        scores = const.tile([P, C], F32)
-        chunk_max = const.tile([P, CHUNKS], F32)
+        for q in range(LAST):
+            if q + TURN_AHEAD < CHUNKS:
+                turn(q + TURN_AHEAD)
+            multiply(q)
+            inverse_mem_norm(q)
+            square_and_quantise(q + 1)
+        score(0, LAST)
+        nc.vector.tensor_reduce(
+            out=scores[:, C : C + 1], in_=scores[:, 0 : LAST * CELLS], axis=AXIS.X, op=ALU.max
+        )
+        multiply(LAST)
+        inverse_mem_norm(LAST)
+        score(LAST, CHUNKS)
         next_table = const.tile([P, 1], F32)
-
-        for q in range(CHUNKS):
-            words = cells_sb[q][:].bitcast(F32)
-            mem_vals = chunk.tile([P, B, P, T * PACK], BF16, name="mem_vals", align_bytes=64)
-            sq_vals = chunk.tile([P, B, P, T * PACK], BF16, name="sq_vals", align_bytes=64)
-            for b in range(B):
-                turned = flip.tile([P, PACK, P], F32, name="turned")
-                for m in range(T * 2):
-                    nc.tensor.transpose(
-                        turned[:, m, :], words[:, b, m * P : (m + 1) * P], ident[:]
-                    )
-                nc.scalar.copy(
-                    out=mem_vals[:].bitcast(F32)[:, b, :, :],
-                    in_=turned[:].rearrange("p m j -> p j m"),
-                )
-                if b == 0:
-                    nc.vector.tensor_mul(
-                        out=sq_vals[:, b, :, :], in0=mem_vals[:, b, :, :], in1=mem_vals[:, b, :, :]
-                    )
-                else:
-                    nc.scalar.activation(
-                        out=sq_vals[:, b, :, :].rearrange("p j (m e) -> p j m e", e=2),
-                        in_=turned[:].bitcast(BF16).rearrange("p m (j e) -> p j m e", e=2),
-                        func=ACT.Square,
-                    )
-
-            acc = sums.tile([P, 2, CELLS], F32, name="acc")
-            for o, vals in enumerate((mem_vals, sq_vals)):
-                codes = chunk.tile([P, B * CELLS], U32, name="codes%d" % o, align_bytes=64)
-                scales = chunk.tile([P, B * CELLS], U8, name="scales%d" % o, align_bytes=64)
-                nc.vector.quantize_mx(
-                    out=codes[:].bitcast(FP8X4),
-                    scales=scales[:],
-                    in_=vals[:].rearrange("p b j v -> p (b j v)"),
-                )
-                for b in range(B):
-                    heads = slice(o * 4 * H + b * H, o * 4 * H + b * H + P)
-                    cols = slice(b * CELLS, (b + 1) * CELLS)
-                    nc.tensor.matmul_mx(
-                        out=acc[:, o, :],
-                        lhsT=head_codes[:, heads].bitcast(FP8X4),
-                        lhsT_scale=head_scales[:, heads],
-                        rhs=codes[:, cols].bitcast(FP8X4),
-                        rhs_scale=scales[:, cols],
-                        start=(b == 0),
-                        stop=(b == B - 1),
-                    )
-
-            a = chunk.tile([P, CELLS], F32, name="a")
-            nc.scalar.activation(
-                out=a[:], in_=acc[:, 1, :], func=ACT.Abs_reciprocal_sqrt, bias=guard[:]
-            )
-            den_sq = chunk.tile([P, CELLS], F32, name="den_sq")
-            nc.scalar.activation(
-                out=den_sq[:], in_=a[:], func=ACT.Square, scale=EPS, bias=keys_norm[:]
-            )
-            u = chunk.tile([P, CELLS], F32, name="u")
-            nc.scalar.activation(out=u[:], in_=den_sq[:], func=ACT.Abs_reciprocal_sqrt)
-            if q == CHUNKS - 1:
-                nc.scalar.activation(out=next_table[:], in_=u[:, 0:1], func=ACT.Exp)
-            cosine = chunk.tile([P, CELLS], F32, name="cosine")
-            nc.vector.scalar_tensor_tensor(
-                out=cosine[:], in0=acc[:, 0, :], scalar=beta[:, 0:1], in1=a[:],
-                op0=ALU.mult, op1=ALU.mult,
-            )
-            cols = slice(q * CELLS, (q + 1) * CELLS)
-            nc.vector.tensor_mul(out=scores[:, cols], in0=cosine[:], in1=u[:])
-            nc.vector.tensor_reduce(
-                out=chunk_max[:, q : q + 1], in_=scores[:, cols], axis=AXIS.X, op=ALU.max
-            )
+        nc.scalar.activation(out=next_table[:], in_=inv_den[:, C - 1 : C], func=ACT.Exp)
 
         neg_max = const.tile([P, 1], F32)
         nc.vector.tensor_reduce(
-            out=neg_max[:], in_=chunk_max[:], axis=AXIS.X, op=ALU.max, negate=True
+            out=neg_max[:], in_=scores[:, LAST * CELLS : C + 1], axis=AXIS.X, op=ALU.max, negate=True
         )
         expd = const.tile([P, C], F32)
         total = const.tile([P, 1], F32)
         nc.scalar.activation(
-            out=expd[:], in_=scores[:], func=ACT.Exp, bias=neg_max[:], accum_out=total[:]
+            out=expd[:], in_=scores[:, 0:C], func=ACT.Exp, bias=neg_max[:], accum_out=total[:]
         )
         inv_total = const.tile([P, 1], F32)
         nc.vector.reciprocal(out=inv_total[:], in_=total[:])
         out_rows = out.rearrange("b h c -> (b h) c")
-        half = C // 2
-        left = const.tile([P, half], F32)
-        nc.vector.tensor_scalar_mul(out=left[:], in0=expd[:, 0:half], scalar1=inv_total[:, 0:1])
-        nc.sync.dma_start(out=out_rows[:, 0:half], in_=left[:])
-        right = const.tile([P, half], F32)
-        nc.scalar.activation(out=right[:], in_=expd[:, half:C], func=ACT.Copy, scale=inv_total[:, 0:1])
-        nc.scalar.dma_start(out=out_rows[:, half:C], in_=right[:])
+        left = const.tile([P, VECTOR_COLS], F32)
+        nc.vector.tensor_scalar_mul(
+            out=left[:], in0=expd[:, 0:VECTOR_COLS], scalar1=inv_total[:, 0:1]
+        )
+        nc.sync.dma_start(out=out_rows[:, 0:VECTOR_COLS], in_=left[:])
+        right = const.tile([P, C - VECTOR_COLS], F32)
+        nc.scalar.activation(
+            out=right[:], in_=expd[:, VECTOR_COLS:C], func=ACT.Copy, scale=inv_total[:, 0:1]
+        )
+        nc.scalar.dma_start(out=out_rows[:, VECTOR_COLS:C], in_=right[:])

@@ -23,6 +23,7 @@ T = 2
 CELLS = T * P
 CHUNKS = C // CELLS
 LAST = CHUNKS - 1
+HALF = CHUNKS // 2
 TURN_AHEAD = 2
 VECTOR_COLS = 640
 
@@ -64,8 +65,8 @@ def tile_contentaddressing_s_kernel(tc, memory, keys, betas, mask, out):
         for q in range(1, CHUNKS):
             nc.sync.dma_start(out=cells_sb[q][:], in_=mem_view[q])
 
-        mem_vals = [
-            chunk.tile([P, B, P, T * PACK], BF16, name="mem_vals", align_bytes=64)
+        vals = [
+            chunk.tile([P, 2, B, P, T * PACK], BF16, name="vals", align_bytes=64)
             for q in range(CHUNKS)
         ]
         codes = {}
@@ -86,33 +87,44 @@ def tile_contentaddressing_s_kernel(tc, memory, keys, betas, mask, out):
                         turned[:, m, :], words[:, b, m * P : (m + 1) * P], ident[:]
                     )
                 nc.scalar.copy(
-                    out=mem_vals[q][:].bitcast(F32)[:, b, :, :],
+                    out=vals[q][:].bitcast(F32)[:, 0, b, :, :],
                     in_=turned[:].rearrange("p m j -> p j m"),
                 )
-
-        def square_and_quantise(q):
-            flat = mem_vals[q][:].rearrange("p b j v -> p (b j v)")
-            sq_vals = chunk.tile([P, B * CELLS * PACK], BF16, name="sq_vals", align_bytes=64)
-            nc.vector.tensor_mul(out=sq_vals[:], in0=flat, in1=flat)
-            for o, vals in enumerate((flat, sq_vals[:])):
-                codes[q, o] = chunk.tile([P, B * CELLS], U32, name="codes%d" % o, align_bytes=64)
-                scales[q, o] = chunk.tile([P, B * CELLS], U8, name="scales%d" % o, align_bytes=64)
-                nc.vector.quantize_mx(
-                    out=codes[q, o][:].bitcast(FP8X4), scales=scales[q, o][:], in_=vals
+            if q >= HALF:
+                nc.scalar.activation(
+                    out=vals[q][:, 1, B - 1, :, :].rearrange("p j (m e) -> p j m e", e=2),
+                    in_=turned[:].bitcast(BF16).rearrange("p m (j e) -> p j m e", e=2),
+                    func=ACT.Square,
                 )
+
+        def square(q):
+            own = B - 1 if q >= HALF else B
+            nc.vector.tensor_mul(
+                out=vals[q][:, 1, 0:own, :, :], in0=vals[q][:, 0, 0:own, :, :],
+                in1=vals[q][:, 0, 0:own, :, :],
+            )
+
+        def quantise(q):
+            codes[q] = chunk.tile([P, 2 * B * CELLS], U32, name="codes", align_bytes=64)
+            scales[q] = chunk.tile([P, 2 * B * CELLS], U8, name="scales", align_bytes=64)
+            nc.vector.quantize_mx(
+                out=codes[q][:].bitcast(FP8X4),
+                scales=scales[q][:],
+                in_=vals[q][:].rearrange("p k b j v -> p (k b j v)"),
+            )
 
         def multiply(q):
             acc[q] = sums.tile([P, 2, CELLS], F32, name="acc")
-            for o in range(2):
+            for o in (1, 0):
                 for b in range(B):
                     heads = slice(o * 4 * H + b * H, o * 4 * H + b * H + P)
-                    cols = slice(b * CELLS, (b + 1) * CELLS)
+                    cols = slice((o * B + b) * CELLS, (o * B + b + 1) * CELLS)
                     nc.tensor.matmul_mx(
                         out=acc[q][:, o, :],
                         lhsT=head_codes[:, heads].bitcast(FP8X4),
                         lhsT_scale=head_scales[:, heads],
-                        rhs=codes[q, o][:, cols].bitcast(FP8X4),
-                        rhs_scale=scales[q, o][:, cols],
+                        rhs=codes[q][:, cols].bitcast(FP8X4),
+                        rhs_scale=scales[q][:, cols],
                         start=(b == 0),
                         stop=(b == B - 1),
                     )
@@ -123,7 +135,7 @@ def tile_contentaddressing_s_kernel(tc, memory, keys, betas, mask, out):
                 func=ACT.Abs_reciprocal_sqrt, bias=guard[:],
             )
 
-        def score(first, stop):
+        def inverse_denominator(first, stop):
             cols = slice(first * CELLS, stop * CELLS)
             nc.scalar.activation(
                 out=den_sq[:, cols], in_=inv_mem[:, cols], func=ACT.Square,
@@ -132,6 +144,9 @@ def tile_contentaddressing_s_kernel(tc, memory, keys, betas, mask, out):
             nc.scalar.activation(
                 out=inv_den[:, cols], in_=den_sq[:, cols], func=ACT.Abs_reciprocal_sqrt
             )
+
+        def score(first, stop):
+            cols = slice(first * CELLS, stop * CELLS)
             for q in range(first, stop):
                 own = slice(q * CELLS, (q + 1) * CELLS)
                 nc.vector.scalar_tensor_tensor(
@@ -146,8 +161,6 @@ def tile_contentaddressing_s_kernel(tc, memory, keys, betas, mask, out):
         nc.vector.tensor_mul(out=m2[:], in0=mask_sb[:], in1=mask_sb[:])
         km2 = const.tile([P, W], F32)
         nc.vector.tensor_mul(out=km2[:], in0=keys_sb[:], in1=m2[:])
-        km = const.tile([P, W], F32)
-        nc.vector.tensor_mul(out=km[:], in0=keys_sb[:], in1=mask_sb[:])
 
         head_view = head_vals[:].rearrange(
             "p (o a z h t) -> p o a z h t", o=2, a=B, z=2, h=H, t=PACK
@@ -163,41 +176,52 @@ def tile_contentaddressing_s_kernel(tc, memory, keys, betas, mask, out):
                 in_=turned[:].rearrange("p t (a h) -> p a h t", a=B),
             )
 
+        square(0)
+        turn(1)
+
         km_sq = const.tile([P, W], F32)
         kn_sq = const.tile([P, 1], F32)
-        nc.scalar.activation(out=km_sq[:], in_=km[:], func=ACT.Square, accum_out=kn_sq[:])
+        nc.vector.scalar_tensor_tensor(
+            out=km_sq[:], in0=keys_sb[:], scalar=1.0, in1=km2[:], op0=ALU.mult, op1=ALU.mult,
+            accum_out=kn_sq[:],
+        )
         kn_inv = const.tile([P, 1], F32)
         nc.scalar.activation(
             out=kn_inv[:], in_=kn_sq[:], func=ACT.Abs_reciprocal_sqrt, bias=guard[:]
         )
 
-        turn(1)
-        square_and_quantise(0)
+        quantise(0)
         head_codes = const.tile([P, 2 * B * 2 * H], U32, align_bytes=64)
         head_scales = const.tile([P, 2 * B * 2 * H], U8, align_bytes=64)
         nc.vector.quantize_mx(
             out=head_codes[:].bitcast(FP8X4), scales=head_scales[:], in_=head_vals[:]
         )
+        square(1)
         keys_norm = const.tile([P, 1], F32)
         nc.vector.reciprocal(out=keys_norm[:], in_=kn_inv[:])
         beta = const.tile([P, 1], F32)
         nc.vector.tensor_copy(out=beta[:], in_=beta_bf[:])
 
-        for q in range(LAST):
-            if q + TURN_AHEAD < CHUNKS:
-                turn(q + TURN_AHEAD)
+        for q in range(HALF):
+            turn(q + TURN_AHEAD)
             multiply(q)
             inverse_mem_norm(q)
-            square_and_quantise(q + 1)
+            square(q + TURN_AHEAD)
+            quantise(q + 1)
+        inverse_denominator(0, HALF)
+        for q in range(HALF, CHUNKS):
+            multiply(q)
+            inverse_mem_norm(q)
+            inverse_denominator(q, q + 1)
+            if q < LAST:
+                quantise(q + 1)
+        next_table = const.tile([P, 1], F32)
+        nc.scalar.activation(out=next_table[:], in_=inv_den[:, C - 1 : C], func=ACT.Exp)
         score(0, LAST)
         nc.vector.tensor_reduce(
             out=scores[:, C : C + 1], in_=scores[:, 0 : LAST * CELLS], axis=AXIS.X, op=ALU.max
         )
-        multiply(LAST)
-        inverse_mem_norm(LAST)
         score(LAST, CHUNKS)
-        next_table = const.tile([P, 1], F32)
-        nc.scalar.activation(out=next_table[:], in_=inv_den[:, C - 1 : C], func=ACT.Exp)
 
         neg_max = const.tile([P, 1], F32)
         nc.vector.tensor_reduce(

@@ -65,8 +65,12 @@ def tile_contentaddressing_s_kernel(tc, memory, keys, betas, mask, out):
         for q in range(1, CHUNKS):
             nc.sync.dma_start(out=cells_sb[q][:], in_=mem_view[q])
 
-        vals = [
-            chunk.tile([P, 2, B, P, T * PACK], BF16, name="vals", align_bytes=64)
+        mem_vals = [
+            chunk.tile([P, B, P, T * PACK], BF16, name="mem_vals", align_bytes=64)
+            for q in range(CHUNKS)
+        ]
+        sq_vals = [
+            chunk.tile([P, B * CELLS * PACK], BF16, name="sq_vals", align_bytes=64)
             for q in range(CHUNKS)
         ]
         codes = {}
@@ -87,44 +91,38 @@ def tile_contentaddressing_s_kernel(tc, memory, keys, betas, mask, out):
                         turned[:, m, :], words[:, b, m * P : (m + 1) * P], ident[:]
                     )
                 nc.scalar.copy(
-                    out=vals[q][:].bitcast(F32)[:, 0, b, :, :],
+                    out=mem_vals[q][:].bitcast(F32)[:, b, :, :],
                     in_=turned[:].rearrange("p m j -> p j m"),
                 )
-            if q >= HALF:
+            if q == LAST:
                 nc.scalar.activation(
-                    out=vals[q][:, 1, B - 1, :, :].rearrange("p j (m e) -> p j m e", e=2),
-                    in_=turned[:].bitcast(BF16).rearrange("p m (j e) -> p j m e", e=2),
+                    out=sq_vals[q][:], in_=mem_vals[q][:].rearrange("p b j v -> p (b j v)"),
                     func=ACT.Square,
                 )
 
-        def square(q):
-            own = B - 1 if q >= HALF else B
-            nc.vector.tensor_mul(
-                out=vals[q][:, 1, 0:own, :, :], in0=vals[q][:, 0, 0:own, :, :],
-                in1=vals[q][:, 0, 0:own, :, :],
-            )
-
-        def quantise(q):
-            codes[q] = chunk.tile([P, 2 * B * CELLS], U32, name="codes", align_bytes=64)
-            scales[q] = chunk.tile([P, 2 * B * CELLS], U8, name="scales", align_bytes=64)
-            nc.vector.quantize_mx(
-                out=codes[q][:].bitcast(FP8X4),
-                scales=scales[q][:],
-                in_=vals[q][:].rearrange("p k b j v -> p (k b j v)"),
-            )
+        def square_and_quantise(q):
+            flat = mem_vals[q][:].rearrange("p b j v -> p (b j v)")
+            if q < LAST:
+                nc.vector.tensor_mul(out=sq_vals[q][:], in0=flat, in1=flat)
+            for o, vals in enumerate((flat, sq_vals[q][:])):
+                codes[q, o] = chunk.tile([P, B * CELLS], U32, name="codes%d" % o, align_bytes=64)
+                scales[q, o] = chunk.tile([P, B * CELLS], U8, name="scales%d" % o, align_bytes=64)
+                nc.vector.quantize_mx(
+                    out=codes[q, o][:].bitcast(FP8X4), scales=scales[q, o][:], in_=vals
+                )
 
         def multiply(q):
             acc[q] = sums.tile([P, 2, CELLS], F32, name="acc")
             for o in (1, 0):
                 for b in range(B):
                     heads = slice(o * 4 * H + b * H, o * 4 * H + b * H + P)
-                    cols = slice((o * B + b) * CELLS, (o * B + b + 1) * CELLS)
+                    cols = slice(b * CELLS, (b + 1) * CELLS)
                     nc.tensor.matmul_mx(
                         out=acc[q][:, o, :],
                         lhsT=head_codes[:, heads].bitcast(FP8X4),
                         lhsT_scale=head_scales[:, heads],
-                        rhs=codes[q][:, cols].bitcast(FP8X4),
-                        rhs_scale=scales[q][:, cols],
+                        rhs=codes[q, o][:, cols].bitcast(FP8X4),
+                        rhs_scale=scales[q, o][:, cols],
                         start=(b == 0),
                         stop=(b == B - 1),
                     )
@@ -161,6 +159,12 @@ def tile_contentaddressing_s_kernel(tc, memory, keys, betas, mask, out):
         nc.vector.tensor_mul(out=m2[:], in0=mask_sb[:], in1=mask_sb[:])
         km2 = const.tile([P, W], F32)
         nc.vector.tensor_mul(out=km2[:], in0=keys_sb[:], in1=m2[:])
+        km_sq = const.tile([P, W], F32)
+        kn_sq = const.tile([P, 1], F32)
+        nc.vector.scalar_tensor_tensor(
+            out=km_sq[:], in0=keys_sb[:], scalar=1.0, in1=km2[:], op0=ALU.mult, op1=ALU.mult,
+            accum_out=kn_sq[:],
+        )
 
         head_view = head_vals[:].rearrange(
             "p (o a z h t) -> p o a z h t", o=2, a=B, z=2, h=H, t=PACK
@@ -176,27 +180,18 @@ def tile_contentaddressing_s_kernel(tc, memory, keys, betas, mask, out):
                 in_=turned[:].rearrange("p t (a h) -> p a h t", a=B),
             )
 
-        square(0)
-        turn(1)
-
-        km_sq = const.tile([P, W], F32)
-        kn_sq = const.tile([P, 1], F32)
-        nc.vector.scalar_tensor_tensor(
-            out=km_sq[:], in0=keys_sb[:], scalar=1.0, in1=km2[:], op0=ALU.mult, op1=ALU.mult,
-            accum_out=kn_sq[:],
-        )
         kn_inv = const.tile([P, 1], F32)
         nc.scalar.activation(
             out=kn_inv[:], in_=kn_sq[:], func=ACT.Abs_reciprocal_sqrt, bias=guard[:]
         )
 
-        quantise(0)
+        turn(1)
+        square_and_quantise(0)
         head_codes = const.tile([P, 2 * B * 2 * H], U32, align_bytes=64)
         head_scales = const.tile([P, 2 * B * 2 * H], U8, align_bytes=64)
         nc.vector.quantize_mx(
             out=head_codes[:].bitcast(FP8X4), scales=head_scales[:], in_=head_vals[:]
         )
-        square(1)
         keys_norm = const.tile([P, 1], F32)
         nc.vector.reciprocal(out=keys_norm[:], in_=kn_inv[:])
         beta = const.tile([P, 1], F32)
@@ -206,26 +201,25 @@ def tile_contentaddressing_s_kernel(tc, memory, keys, betas, mask, out):
             turn(q + TURN_AHEAD)
             multiply(q)
             inverse_mem_norm(q)
-            square(q + TURN_AHEAD)
-            quantise(q + 1)
+            square_and_quantise(q + 1)
         inverse_denominator(0, HALF)
         for q in range(HALF, CHUNKS):
             multiply(q)
             inverse_mem_norm(q)
-            inverse_denominator(q, q + 1)
             if q < LAST:
-                quantise(q + 1)
+                square_and_quantise(q + 1)
+        inverse_denominator(HALF, CHUNKS)
         next_table = const.tile([P, 1], F32)
         nc.scalar.activation(out=next_table[:], in_=inv_den[:, C - 1 : C], func=ACT.Exp)
-        score(0, LAST)
+        score(0, HALF)
         nc.vector.tensor_reduce(
-            out=scores[:, C : C + 1], in_=scores[:, 0 : LAST * CELLS], axis=AXIS.X, op=ALU.max
+            out=scores[:, C : C + 1], in_=scores[:, 0 : HALF * CELLS], axis=AXIS.X, op=ALU.max
         )
-        score(LAST, CHUNKS)
+        score(HALF, CHUNKS)
 
         neg_max = const.tile([P, 1], F32)
         nc.vector.tensor_reduce(
-            out=neg_max[:], in_=scores[:, LAST * CELLS : C + 1], axis=AXIS.X, op=ALU.max, negate=True
+            out=neg_max[:], in_=scores[:, HALF * CELLS : C + 1], axis=AXIS.X, op=ALU.max, negate=True
         )
         expd = const.tile([P, C], F32)
         total = const.tile([P, 1], F32)

from contextlib import ExitStack

import concourse.mybir as mybir
from concourse.masks import make_identity

F32 = mybir.dt.float32
BF16 = mybir.dt.bfloat16
I32 = mybir.dt.int32
U32 = mybir.dt.uint32
U8 = mybir.dt.uint8
FP8X4 = mybir.dt.float8_e4m3fn_x4
ACT = mybir.ActivationFunctionType
ALU = mybir.AluOpType
AXIS = mybir.AxisListType

B, H, C, W = 2, 64, 1024, 512
P = 128
PACK = 4
EPS = 1e-8
GUARD = 1e-26

T = 2
CELLS = T * P
CHUNKS = C // CELLS
LAST = CHUNKS - 1
HALF = CHUNKS // 2
TURN_AHEAD = 2
VECTOR_COLS = 640

FLOPS = 2 * 2 * B * H * C * W

assert B * H == P and W == P * PACK


def tile_contentaddressing_s_kernel(tc, memory, keys, betas, mask, out):
    nc = tc.nc
    with ExitStack() as stack:
        const = stack.enter_context(tc.tile_pool(name="const", bufs=1))
        chunk = stack.enter_context(tc.tile_pool(name="chunk", bufs=CHUNKS))
        flip = stack.enter_context(tc.psum_pool(name="flip", bufs=2 * TURN_AHEAD))
        sums = stack.enter_context(tc.psum_pool(name="sums", bufs=CHUNKS))
        stack.enter_context(tc.manual_schedule())

        beta_bf = const.tile([P, 1], BF16)
        with nc.allow_non_contiguous_dma(reason="one beta for each partition, 128 in all"):
            nc.scalar.dma_start(out=beta_bf[:], in_=betas.rearrange("b (h o) -> (b h) o", o=1))

        ident = const.tile([P, P], F32)
        make_identity(nc, ident[:])
        guard = const.tile([P, 1], F32)
        nc.vector.memset(guard[:], GUARD)
        first_table = const.tile([P, 1], F32)
        nc.scalar.activation(out=first_table[:], in_=guard[:], func=ACT.Abs_reciprocal_sqrt)
        head_vals = const.tile([P, 2 * B * 2 * H * PACK], BF16, align_bytes=64)
        nc.vector.memset(head_vals[:].bitcast(I32), 0)

        mem_view = memory.rearrange("b (q j t) w -> q j b (t w)", q=CHUNKS, j=P, t=T)
        cells_sb = [chunk.tile([P, B, T * W], BF16, name="x") for q in range(CHUNKS)]
        mask_sb = const.tile([P, W], BF16)
        keys_sb = const.tile([P, W], BF16)
        nc.sync.dma_start(out=cells_sb[0][:, 0, :], in_=mem_view[0][:, 0, :])
        nc.sync.dma_start(out=mask_sb[:], in_=mask.rearrange("b h w -> (b h) w"))
        nc.sync.dma_start(out=keys_sb[:], in_=keys.rearrange("b h w -> (b h) w"))
        nc.sync.dma_start(out=cells_sb[0][:, 1, :], in_=mem_view[0][:, 1, :])
        for q in range(1, CHUNKS):
            nc.sync.dma_start(out=cells_sb[q][:], in_=mem_view[q])

        mem_vals = [
            chunk.tile([P, B, P, T * PACK], BF16, name="mem_vals", align_bytes=64)
            for q in range(CHUNKS)
        ]
        sq_vals = [
            chunk.tile([P, B * CELLS * PACK], BF16, name="sq_vals", align_bytes=64)
            for q in range(CHUNKS)
        ]
        codes = {}
        scales = {}
        acc = {}
        inv_mem = const.tile([P, C], F32)
        den_sq = const.tile([P, C], F32)
        inv_den = const.tile([P, C], F32)
        cosine = const.tile([P, C], F32)
        scores = const.tile([P, C + 1], F32)

        def turn(q):
            words = cells_sb[q][:].bitcast(F32)
            for b in range(B):
                turned = flip.tile([P, PACK, P], F32, name="turned")
                for m in range(T * 2):
                    nc.tensor.transpose(
                        turned[:, m, :], words[:, b, m * P : (m + 1) * P], ident[:]
                    )
                nc.scalar.copy(
                    out=mem_vals[q][:].bitcast(F32)[:, b, :, :],
                    in_=turned[:].rearrange("p m j -> p j m"),
                )
            if q == LAST:
                nc.scalar.activation(
                    out=sq_vals[q][:], in_=mem_vals[q][:].rearrange("p b j v -> p (b j v)"),
                    func=ACT.Square,
                )

        def square_and_quantise(q):
            flat = mem_vals[q][:].rearrange("p b j v -> p (b j v)")
            if q < LAST:
                nc.vector.tensor_mul(out=sq_vals[q][:], in0=flat, in1=flat)
            for o, vals in enumerate((flat, sq_vals[q][:])):
                codes[q, o] = chunk.tile([P, B * CELLS], U32, name="codes%d" % o, align_bytes=64)
                scales[q, o] = chunk.tile([P, B * CELLS], U8, name="scales%d" % o, align_bytes=64)
                nc.vector.quantize_mx(
                    out=codes[q, o][:].bitcast(FP8X4), scales=scales[q, o][:], in_=vals
                )

        def multiply(q):
            acc[q] = sums.tile([P, 2, CELLS], F32, name="acc")
            for o in (1, 0):
                for b in range(B):
                    heads = slice(o * 4 * H + b * H, o * 4 * H + b * H + P)
                    cols = slice(b * CELLS, (b + 1) * CELLS)
                    nc.tensor.matmul_mx(
                        out=acc[q][:, o, :],
                        lhsT=head_codes[:, heads].bitcast(FP8X4),
                        lhsT_scale=head_scales[:, heads],
                        rhs=codes[q, o][:, cols].bitcast(FP8X4),
                        rhs_scale=scales[q, o][:, cols],
                        start=(b == 0),
                        stop=(b == B - 1),
                    )

        def inverse_mem_norm(q):
            nc.scalar.activation(
                out=inv_mem[:, q * CELLS : (q + 1) * CELLS], in_=acc[q][:, 1, :],
                func=ACT.Abs_reciprocal_sqrt, bias=guard[:],
            )

        def inverse_denominator(first, stop):
            cols = slice(first * CELLS, stop * CELLS)
            nc.scalar.activation(
                out=den_sq[:, cols], in_=inv_mem[:, cols], func=ACT.Square,
                scale=EPS, bias=keys_norm[:],
            )
            nc.scalar.activation(
                out=inv_den[:, cols], in_=den_sq[:, cols], func=ACT.Abs_reciprocal_sqrt
            )

        def score(first, stop):
            cols = slice(first * CELLS, stop * CELLS)
            for q in range(first, stop):
                own = slice(q * CELLS, (q + 1) * CELLS)
                nc.vector.scalar_tensor_tensor(
                    out=cosine[:, own], in0=acc[q][:, 0, :], scalar=beta[:, 0:1],
                    in1=inv_mem[:, own], op0=ALU.mult, op1=ALU.mult,
                )
            nc.vector.tensor_mul(out=scores[:, cols], in0=cosine[:, cols], in1=inv_den[:, cols])

        turn(0)

        m2 = const.tile([P, W], F32)
        nc.vector.tensor_mul(out=m2[:], in0=mask_sb[:], in1=mask_sb[:])
        km2 = const.tile([P, W], F32)
        nc.vector.tensor_mul(out=km2[:], in0=keys_sb[:], in1=m2[:])
        km_sq = const.tile([P, W], F32)
        kn_sq = const.tile([P, 1], F32)
        nc.vector.scalar_tensor_tensor(
            out=km_sq[:], in0=keys_sb[:], scalar=1.0, in1=km2[:], op0=ALU.mult, op1=ALU.mult,
            accum_out=kn_sq[:],
        )

        head_view = head_vals[:].rearrange(
            "p (o a z h t) -> p o a z h t", o=2, a=B, z=2, h=H, t=PACK
        )
        for o, rows in ((1, m2), (0, km2)):
            turned = flip.tile([P, PACK, P], F32, name="turned")
            by_word = rows[:].rearrange("r (u p e) -> r u e p", u=2, e=2)
            for u in range(2):
                for e in range(2):
                    nc.tensor.transpose(turned[:, 2 * u + e, :], by_word[:, u, e, :], ident[:])
            nc.scalar.copy(
                out=head_view[:, o, :, 0, :, :],
                in_=turned[:].rearrange("p t (a h) -> p a h t", a=B),
            )

        kn_inv = const.tile([P, 1], F32)
        nc.scalar.activation(
            out=kn_inv[:], in_=kn_sq[:], func=ACT.Abs_reciprocal_sqrt, bias=guard[:]
        )

        turn(1)
        square_and_quantise(0)
        head_codes = const.tile([P, 2 * B * 2 * H], U32, align_bytes=64)
        head_scales = const.tile([P, 2 * B * 2 * H], U8, align_bytes=64)
        nc.vector.quantize_mx(
            out=head_codes[:].bitcast(FP8X4), scales=head_scales[:], in_=head_vals[:]
        )
        keys_norm = const.tile([P, 1], F32)
        nc.vector.reciprocal(out=keys_norm[:], in_=kn_inv[:])
        beta = const.tile([P, 1], F32)
        nc.vector.tensor_copy(out=beta[:], in_=beta_bf[:])

        for q in range(HALF):
            turn(q + TURN_AHEAD)
            multiply(q)
            inverse_mem_norm(q)
            square_and_quantise(q + 1)
        inverse_denominator(0, HALF)
        for q in range(HALF, CHUNKS):
            multiply(q)
            inverse_mem_norm(q)
            if q < LAST:
                square_and_quantise(q + 1)
        inverse_denominator(HALF, CHUNKS)
        next_table = const.tile([P, 1], F32)
        nc.scalar.activation(out=next_table[:], in_=inv_den[:, C - 1 : C], func=ACT.Exp)
        score(0, HALF)
        nc.vector.tensor_reduce(
            out=scores[:, C : C + 1], in_=scores[:, 0 : HALF * CELLS], axis=AXIS.X, op=ALU.max
        )
        score(HALF, CHUNKS)

        neg_max = const.tile([P, 1], F32)
        nc.vector.tensor_reduce(
            out=neg_max[:], in_=scores[:, HALF * CELLS : C + 1], axis=AXIS.X, op=ALU.max, negate=True
        )
        expd = const.tile([P, C], F32)
        total = const.tile([P, 1], F32)
        nc.scalar.activation(
            out=expd[:], in_=scores[:, 0:C], func=ACT.Exp, bias=neg_max[:], accum_out=total[:]
        )
        inv_total = const.tile([P, 1], F32)
        nc.vector.reciprocal(out=inv_total[:], in_=total[:])
        out_rows = out.rearrange("b h c -> (b h) c")
        left = const.tile([P, VECTOR_COLS], F32)
        nc.vector.tensor_scalar_mul(
            out=left[:], in0=expd[:, 0:VECTOR_COLS], scalar1=inv_total[:, 0:1]
        )
        nc.sync.dma_start(out=out_rows[:, 0:VECTOR_COLS], in_=left[:])
        right = const.tile([P, C - VECTOR_COLS], F32)
        nc.scalar.activation(
            out=right[:], in_=expd[:, VECTOR_COLS:C], func=ACT.Copy, scale=inv_total[:, 0:1]
        )
        nc.scalar.dma_start(out=out_rows[:, VECTOR_COLS:C], in_=right[:])
